import numpy as np
import ml_dtypes


def mxq(x, axis, fmt="e4m3"):
    dtype, down = {"e4m3": (ml_dtypes.float8_e4m3fn, 7), "e5m2": (ml_dtypes.float8_e5m2, 14)}[fmt]
    v = np.moveaxis(np.asarray(x, np.float32).astype(ml_dtypes.bfloat16).astype(np.float64), axis, -1)
    blocks = v.reshape(v.shape[:-1] + (-1, 32))
    amax = np.abs(blocks).max(-1, keepdims=True)
    byte = np.maximum(np.where(amax > 0, np.frexp(amax)[1] - 1 + 127, 0) - down, 1)
    scale = np.exp2(byte - 127.0)
    codes = (blocks / scale).astype(np.float32).astype(dtype).astype(np.float64)
    return np.moveaxis((codes * scale).reshape(v.shape), -1, axis)


WIDE = False


def mx_kscale(k):
    if not WIDE:
        return np.ones(k)
    levels = np.array([10, -10, 5, -5, 0])
    a = np.random.permutation(np.resize(levels, k // 512 * 4)).reshape(k // 512, 4)
    idx = np.arange(k)
    return np.exp2(a[idx // 512, idx % 128 // 32])


BF16 = ml_dtypes.bfloat16


def bf(x):
    return np.asarray(x, np.float32).astype(BF16)


def f64(x):
    return np.asarray(x).astype(np.float64)


B, N, I, O = 2, 512, 256, 128


def setup_inputs():
    s = mx_kscale(N)
    limit = np.sqrt(6.0 / (I + O))
    return {"seq": bf(np.random.standard_normal((B, N, I)) / s[None, :, None]),
            "adj": bf(np.random.uniform(0.0, 1.0, (B, N, N)) / np.sqrt(N) * s[None, None, :]),
            "W": bf(np.random.uniform(-limit, limit, (O, I))),
            "b": bf(np.random.standard_normal(O) * 0.1 / s.max()),
            "alpha": bf(0.25 + 0.05 * np.random.standard_normal(1))}


def reference(seq, adj, W, b, alpha):
    h = f64(seq) @ f64(W).T + f64(b)
    h = mxq(f64(adj), 2, "e4m3") @ mxq(h, 1, "e4m3")
    return np.where(h > 0, h, f64(alpha) * h)

@@ -1,0 +1,168 @@
+from contextlib import ExitStack
+
+import concourse.mybir as mybir
+from concourse.masks import make_identity
+
+F32 = mybir.dt.float32
+BF16 = mybir.dt.bfloat16
+U32 = mybir.dt.uint32
+U8 = mybir.dt.uint8
+FP8X4 = mybir.dt.float8_e4m3fn_x4
+ALU = mybir.AluOpType
+ACT = mybir.ActivationFunctionType
+
+P = 128
+PACK = 4
+GRAPHS, NODES, F_IN, F_OUT = 2, 512, 256, 128
+ROW_TILES = NODES // P
+HALVES = 2
+TILES_PER_HALF = ROW_TILES // HALVES
+BANK = 512
+
+FLOPS = 2 * GRAPHS * NODES * F_IN * F_OUT + 2 * GRAPHS * NODES * NODES * F_OUT
+
+
+def tile_gcn_s_kernel(tc, seq, adj, W, b, alpha, out):
+    nc = tc.nc
+    with ExitStack() as ctx:
+        const = ctx.enter_context(tc.tile_pool(name="const", bufs=1))
+        per_graph = ctx.enter_context(tc.tile_pool(name="per_graph", bufs=GRAPHS))
+        per_half = ctx.enter_context(tc.tile_pool(name="per_half", bufs=GRAPHS * HALVES))
+        psum_t = ctx.enter_context(tc.psum_pool(name="psum_t", bufs=3))
+        psum_acc = ctx.enter_context(tc.psum_pool(name="psum_acc", bufs=4))
+        psum_small = ctx.enter_context(tc.psum_pool(name="psum_small", bufs=1))
+
+        ident = const.tile([P, P], F32)
+        make_identity(nc, ident[:])
+        ones = const.tile([P, P], BF16)
+        nc.scalar.activation(out=ones[:], in_=ident[:], func=ACT.Relu, scale=0.0, bias=1.0)
+        small_row = const.tile([P, 2 * F_OUT], BF16)
+        nc.vector.memset(small_row[:], 0.0)
+
+        w_rows = const.tile([P, F_IN], BF16)
+        nc.sync.dma_start(out=w_rows[:], in_=W[:, :])
+        nc.scalar.dma_start(out=small_row[0:1, 0:F_OUT], in_=b.unsqueeze(0))
+        nc.scalar.dma_start(out=small_row[0:1, F_OUT : F_OUT + 1], in_=alpha.unsqueeze(0))
+
+        seq_rows_of = []
+        for g in range(GRAPHS):
+            seq_rows = per_graph.tile([P, PACK * F_IN], BF16)
+            nc.sync.dma_start(
+                out=seq_rows[:].rearrange("p (u r) -> p u r", u=2),
+                in_=seq[g].rearrange("(u p e) i -> p u (e i)", u=2, e=2),
+            )
+            seq_rows_of.append(seq_rows)
+
+        adj_rows_of = []
+        for g in range(GRAPHS):
+            adj_rows = per_graph.tile([P, ROW_TILES * NODES], BF16)
+            adj_view = adj[g].rearrange("(p j) m -> p (j m)", j=ROW_TILES)
+            for half in range(HALVES):
+                cols = slice(half * TILES_PER_HALF * NODES, (half + 1) * TILES_PER_HALF * NODES)
+                nc.sync.dma_start(out=adj_rows[:, cols], in_=adj_view[:, cols])
+            adj_rows_of.append(adj_rows)
+
+        w_t_ps = psum_t.tile([P, BANK], F32, tag="transposed")
+        nc.tensor.transpose(w_t_ps[:, 0:P], w_rows[:].bitcast(F32), ident[:])
+        w_t = const.tile([P, F_OUT], F32)
+        nc.scalar.copy(out=w_t[:], in_=w_t_ps[:, 0:P])
+
+        seq_t_of = []
+        for g in range(GRAPHS):
+            seq_words = seq_rows_of[g][:].bitcast(F32)
+            seq_t_ps = psum_t.tile([P, BANK], F32, tag="transposed")
+            for t in range(PACK):
+                cols = slice(t * P, (t + 1) * P)
+                nc.tensor.transpose(seq_t_ps[:, cols], seq_words[:, cols], ident[:])
+            seq_t = per_graph.tile([P, PACK * P], F32)
+            nc.scalar.copy(out=seq_t[:], in_=seq_t_ps[:])
+            seq_t_of.append(seq_t)
+
+        small_ps = psum_small.tile([P, 2 * F_OUT], F32)
+        nc.tensor.matmul(small_ps[:], lhsT=ones[:], rhs=small_row[:], start=True, stop=True)
+        bias_all = const.tile([P, F_OUT], F32)
+        nc.vector.tensor_copy(out=bias_all[:], in_=small_ps[:, 0:F_OUT])
+        one_minus_alpha = const.tile([P, 1], F32)
+        nc.vector.tensor_scalar(
+            out=one_minus_alpha[:],
+            in0=small_ps[:, F_OUT : F_OUT + 1],
+            scalar1=-1.0,
+            scalar2=1.0,
+            op0=ALU.mult,
+            op1=ALU.add,
+        )
+
+        w_pairs = w_t[:].bitcast(BF16).rearrange("p (o r) -> p o r", r=2)
+        h_codes_of = []
+        h_scales_of = []
+        for g in range(GRAPHS):
+            seq_pairs = seq_t_of[g][:].bitcast(BF16).rearrange("p (t c r) -> p t c r", t=PACK, r=2)
+            h_ps = psum_acc.tile([P, PACK * F_OUT], F32, tag="acc")
+            for t in range(PACK):
+                for r in range(2):
+                    nc.tensor.matmul(
+                        h_ps[:, t * F_OUT : (t + 1) * F_OUT],
+                        lhsT=seq_pairs[:, t, :, r],
+                        rhs=w_pairs[:, :, r],
+                        start=(r == 0),
+                        stop=(r == 1),
+                    )
+            h_grouped = per_graph.tile([P, F_OUT * PACK], BF16, align_bytes=64)
+            nc.vector.tensor_tensor(
+                out=h_grouped[:].rearrange("p (o t) -> p o t", t=PACK),
+                in0=h_ps[:].rearrange("p (t o) -> p o t", t=PACK),
+                in1=bias_all[:].unsqueeze(2).to_broadcast([P, F_OUT, PACK]),
+                op=ALU.add,
+            )
+            h_codes = per_graph.tile([P, F_OUT], U32, align_bytes=64)
+            h_scales = per_graph.tile([P, F_OUT], U8, align_bytes=64)
+            nc.vector.quantize_mx(out=h_codes[:].bitcast(FP8X4), scales=h_scales[:], in_=h_grouped[:])
+            h_codes_of.append(h_codes)
+            h_scales_of.append(h_scales)
+
+        for g in range(GRAPHS):
+            adj_words = adj_rows_of[g][:].bitcast(F32)
+            out_view = out[g].rearrange("(p j) o -> p (j o)", j=ROW_TILES)
+            for half in range(HALVES):
+                adj_t_ps = psum_t.tile([P, BANK], F32, tag="transposed")
+                for k in range(TILES_PER_HALF * 2):
+                    src = (half * TILES_PER_HALF * 2 + k) * P
+                    nc.tensor.transpose(
+                        adj_t_ps[:, k * P : (k + 1) * P], adj_words[:, src : src + P], ident[:]
+                    )
+                adj_grouped = per_half.tile([P, TILES_PER_HALF * P * PACK], BF16, align_bytes=64)
+                nc.scalar.copy(
+                    out=adj_grouped[:].bitcast(F32).rearrange("p (j c u) -> p j c u", j=TILES_PER_HALF, u=2),
+                    in_=adj_t_ps[:].rearrange("p (j u c) -> p j c u", j=TILES_PER_HALF, u=2),
+                )
+                adj_codes = per_half.tile([P, TILES_PER_HALF * P], U32, align_bytes=64)
+                adj_scales = per_half.tile([P, TILES_PER_HALF * P], U8, align_bytes=64)
+                nc.vector.quantize_mx(
+                    out=adj_codes[:].bitcast(FP8X4), scales=adj_scales[:], in_=adj_grouped[:]
+                )
+
+                a_ps = psum_acc.tile([P, TILES_PER_HALF * F_OUT], F32, tag="acc")
+                for j in range(TILES_PER_HALF):
+                    nc.tensor.matmul_mx(
+                        out=a_ps[:, j * F_OUT : (j + 1) * F_OUT],
+                        lhsT=adj_codes[:, j * P : (j + 1) * P].bitcast(FP8X4),
+                        lhsT_scale=adj_scales[:, j * P : (j + 1) * P],
+                        rhs=h_codes_of[g][:].bitcast(FP8X4),
+                        rhs_scale=h_scales_of[g][:],
+                        start=True,
+                        stop=True,
+                    )
+
+                neg_part = per_half.tile([P, TILES_PER_HALF * F_OUT], F32)
+                nc.scalar.activation(out=neg_part[:], in_=a_ps[:], func=ACT.Relu, scale=-1.0)
+                result = per_half.tile([P, TILES_PER_HALF * F_OUT], F32)
+                nc.vector.scalar_tensor_tensor(
+                    out=result[:],
+                    in0=neg_part[:],
+                    scalar=one_minus_alpha[:, 0:1],
+                    in1=a_ps[:],
+                    op0=ALU.mult,
+                    op1=ALU.add,
+                )
+                cols = slice(half * TILES_PER_HALF * F_OUT, (half + 1) * TILES_PER_HALF * F_OUT)
+                nc.sync.dma_start(out=out_view[:, cols], in_=result[:])

@@ -18,6 +18,7 @@ ROW_TILES = NODES // P
 HALVES = 2
 TILES_PER_HALF = ROW_TILES // HALVES
 BANK = 512
+WARM_PASSES = 16
 
 FLOPS = 2 * GRAPHS * NODES * F_IN * F_OUT + 2 * GRAPHS * NODES * NODES * F_OUT
 
@@ -38,6 +39,23 @@ def tile_gcn_s_kernel(tc, seq, adj, W, b, alpha, out):
         nc.scalar.activation(out=ones[:], in_=ident[:], func=ACT.Relu, scale=0.0, bias=1.0)
         small_row = const.tile([P, 2 * F_OUT], BF16)
         nc.vector.memset(small_row[:], 0.0)
+
+        warm_zeros = const.tile([P, P * PACK], BF16, align_bytes=64)
+        nc.vector.memset(warm_zeros[:], 0.0)
+        warm_codes = const.tile([P, P], U32, align_bytes=64)
+        warm_scales = const.tile([P, P], U8, align_bytes=64)
+        nc.vector.quantize_mx(out=warm_codes[:].bitcast(FP8X4), scales=warm_scales[:], in_=warm_zeros[:])
+        warm_ps = psum_t.tile([P, BANK], F32, tag="transposed")
+        for i in range(WARM_PASSES):
+            nc.tensor.matmul_mx(
+                out=warm_ps[:, 0:P],
+                lhsT=warm_codes[:].bitcast(FP8X4),
+                lhsT_scale=warm_scales[:],
+                rhs=warm_codes[:].bitcast(FP8X4),
+                rhs_scale=warm_scales[:],
+                start=True,
+                stop=True,
+            )
 
         w_rows = const.tile([P, F_IN], BF16)
         nc.sync.dma_start(out=w_rows[:], in_=W[:, :])

@@ -15,10 +15,10 @@ P = 128
 PACK = 4
 GRAPHS, NODES, F_IN, F_OUT = 2, 512, 256, 128
 ROW_TILES = NODES // P
-HALVES = 2
-TILES_PER_HALF = ROW_TILES // HALVES
+TILES_PER_HALF = 2
+HALVES = GRAPHS * ROW_TILES // TILES_PER_HALF
 BANK = 512
-WARM_PASSES = 16
+WARM_PASSES = 12
 
 FLOPS = 2 * GRAPHS * NODES * F_IN * F_OUT + 2 * GRAPHS * NODES * NODES * F_OUT
 
@@ -26,19 +26,20 @@ FLOPS = 2 * GRAPHS * NODES * F_IN * F_OUT + 2 * GRAPHS * NODES * NODES * F_OUT
 def tile_gcn_s_kernel(tc, seq, adj, W, b, alpha, out):
     nc = tc.nc
     with ExitStack() as ctx:
+        ctx.enter_context(tc.manual_schedule())
         const = ctx.enter_context(tc.tile_pool(name="const", bufs=1))
         per_graph = ctx.enter_context(tc.tile_pool(name="per_graph", bufs=GRAPHS))
-        per_half = ctx.enter_context(tc.tile_pool(name="per_half", bufs=GRAPHS * HALVES))
+        per_half = ctx.enter_context(tc.tile_pool(name="per_half", bufs=HALVES))
         psum_t = ctx.enter_context(tc.psum_pool(name="psum_t", bufs=3))
         psum_acc = ctx.enter_context(tc.psum_pool(name="psum_acc", bufs=4))
         psum_small = ctx.enter_context(tc.psum_pool(name="psum_small", bufs=1))
 
+        small_row = const.tile([P, 2 * F_OUT], BF16)
+        nc.gpsimd.memset(small_row[:], 0.0)
+        zero_col = const.tile([P, 1], F32)
+        nc.gpsimd.memset(zero_col[:], 0.0)
         ident = const.tile([P, P], F32)
         make_identity(nc, ident[:])
-        ones = const.tile([P, P], BF16)
-        nc.scalar.activation(out=ones[:], in_=ident[:], func=ACT.Relu, scale=0.0, bias=1.0)
-        small_row = const.tile([P, 2 * F_OUT], BF16)
-        nc.vector.memset(small_row[:], 0.0)
 
         warm_zeros = const.tile([P, P * PACK], BF16, align_bytes=64)
         nc.vector.memset(warm_zeros[:], 0.0)
@@ -72,18 +73,23 @@ def tile_gcn_s_kernel(tc, seq, adj, W, b, alpha, out):
             seq_rows_of.append(seq_rows)
 
         adj_rows_of = []
-        for g in range(GRAPHS):
-            adj_rows = per_graph.tile([P, ROW_TILES * NODES], BF16)
-            adj_view = adj[g].rearrange("(p j) m -> p (j m)", j=ROW_TILES)
-            for half in range(HALVES):
-                cols = slice(half * TILES_PER_HALF * NODES, (half + 1) * TILES_PER_HALF * NODES)
-                nc.sync.dma_start(out=adj_rows[:, cols], in_=adj_view[:, cols])
+        for k in range(HALVES):
+            adj_rows = per_half.tile([P, TILES_PER_HALF * NODES], BF16)
+            adj_view = adj[k // 2].rearrange("(p j) m -> p (j m)", j=ROW_TILES)
+            first = (k % 2) * TILES_PER_HALF * NODES
+            nc.sync.dma_start(out=adj_rows[:], in_=adj_view[:, first : first + TILES_PER_HALF * NODES])
             adj_rows_of.append(adj_rows)
+
+        ones = const.tile([P, P], BF16)
+        nc.scalar.activation(
+            out=ones[:], in_=zero_col[:, 0:1].to_broadcast([P, P]), func=ACT.Relu, scale=0.0, bias=1.0
+        )
 
         w_t_ps = psum_t.tile([P, BANK], F32, tag="transposed")
         nc.tensor.transpose(w_t_ps[:, 0:P], w_rows[:].bitcast(F32), ident[:])
         w_t = const.tile([P, F_OUT], F32)
         nc.scalar.copy(out=w_t[:], in_=w_t_ps[:, 0:P])
+        w_pairs = w_t[:].bitcast(BF16).rearrange("p (o r) -> p o r", r=2)
 
         seq_t_of = []
         for g in range(GRAPHS):
@@ -93,7 +99,10 @@ def tile_gcn_s_kernel(tc, seq, adj, W, b, alpha, out):
                 cols = slice(t * P, (t + 1) * P)
                 nc.tensor.transpose(seq_t_ps[:, cols], seq_words[:, cols], ident[:])
             seq_t = per_graph.tile([P, PACK * P], F32)
-            nc.scalar.copy(out=seq_t[:], in_=seq_t_ps[:])
+            if g == 0:
+                nc.vector.tensor_copy(out=seq_t[:], in_=seq_t_ps[:])
+            else:
+                nc.scalar.copy(out=seq_t[:], in_=seq_t_ps[:])
             seq_t_of.append(seq_t)
 
         small_ps = psum_small.tile([P, 2 * F_OUT], F32)
@@ -110,10 +119,14 @@ def tile_gcn_s_kernel(tc, seq, adj, W, b, alpha, out):
             op1=ALU.add,
         )
 
-        w_pairs = w_t[:].bitcast(BF16).rearrange("p (o r) -> p o r", r=2)
+        h_grouped_of = []
         h_codes_of = []
         h_scales_of = []
-        for g in range(GRAPHS):
+        adj_grouped_of = []
+        adj_codes_of = []
+        adj_scales_of = []
+
+        def project(g):
             seq_pairs = seq_t_of[g][:].bitcast(BF16).rearrange("p (t c r) -> p t c r", t=PACK, r=2)
             h_ps = psum_acc.tile([P, PACK * F_OUT], F32, tag="acc")
             for t in range(PACK):
@@ -132,55 +145,73 @@ def tile_gcn_s_kernel(tc, seq, adj, W, b, alpha, out):
                 in1=bias_all[:].unsqueeze(2).to_broadcast([P, F_OUT, PACK]),
                 op=ALU.add,
             )
+            h_grouped_of.append(h_grouped)
+
+        def transpose_adj(k):
+            adj_words = adj_rows_of[k][:].bitcast(F32)
+            adj_t_ps = psum_t.tile([P, BANK], F32, tag="transposed")
+            for block in range(TILES_PER_HALF * 2):
+                cols = slice(block * P, (block + 1) * P)
+                nc.tensor.transpose(adj_t_ps[:, cols], adj_words[:, cols], ident[:])
+            adj_grouped = per_half.tile([P, TILES_PER_HALF * P * PACK], BF16, align_bytes=64)
+            nc.scalar.copy(
+                out=adj_grouped[:].bitcast(F32).rearrange("p (j c u) -> p j c u", j=TILES_PER_HALF, u=2),
+                in_=adj_t_ps[:].rearrange("p (j u c) -> p j c u", j=TILES_PER_HALF, u=2),
+            )
+            adj_grouped_of.append(adj_grouped)
+
+        def quantise_h(g):
             h_codes = per_graph.tile([P, F_OUT], U32, align_bytes=64)
             h_scales = per_graph.tile([P, F_OUT], U8, align_bytes=64)
-            nc.vector.quantize_mx(out=h_codes[:].bitcast(FP8X4), scales=h_scales[:], in_=h_grouped[:])
+            nc.vector.quantize_mx(
+                out=h_codes[:].bitcast(FP8X4), scales=h_scales[:], in_=h_grouped_of[g][:]
+            )
             h_codes_of.append(h_codes)
             h_scales_of.append(h_scales)
 
-        for g in range(GRAPHS):
-            adj_words = adj_rows_of[g][:].bitcast(F32)
+        def quantise_adj(k):
+            adj_codes = per_half.tile([P, TILES_PER_HALF * P], U32, align_bytes=64)
+            adj_scales = per_half.tile([P, TILES_PER_HALF * P], U8, align_bytes=64)
+            nc.vector.quantize_mx(
+                out=adj_codes[:].bitcast(FP8X4), scales=adj_scales[:], in_=adj_grouped_of[k][:]
+            )
+            adj_codes_of.append(adj_codes)
+            adj_scales_of.append(adj_scales)
+
+        for k in range(HALVES):
+            if k < GRAPHS:
+                project(k)
+            transpose_adj(k)
+            if k >= 1:
+                if k - 1 < GRAPHS:
+                    quantise_h(k - 1)
+                quantise_adj(k - 1)
+        quantise_adj(HALVES - 1)
+
+        for k in range(HALVES):
+            g = k // 2
+            a_ps = psum_acc.tile([P, TILES_PER_HALF * F_OUT], F32, tag="acc")
+            for j in range(TILES_PER_HALF):
+                nc.tensor.matmul_mx(
+                    out=a_ps[:, j * F_OUT : (j + 1) * F_OUT],
+                    lhsT=adj_codes_of[k][:, j * P : (j + 1) * P].bitcast(FP8X4),
+                    lhsT_scale=adj_scales_of[k][:, j * P : (j + 1) * P],
+                    rhs=h_codes_of[g][:].bitcast(FP8X4),
+                    rhs_scale=h_scales_of[g][:],
+                    start=True,
+                    stop=True,
+                )
+            neg_part = per_half.tile([P, TILES_PER_HALF * F_OUT], F32)
+            nc.scalar.activation(out=neg_part[:], in_=a_ps[:], func=ACT.Relu, scale=-1.0)
+            result = per_half.tile([P, TILES_PER_HALF * F_OUT], F32)
+            nc.vector.scalar_tensor_tensor(
+                out=result[:],
+                in0=neg_part[:],
+                scalar=one_minus_alpha[:, 0:1],
+                in1=a_ps[:],
+                op0=ALU.mult,
+                op1=ALU.add,
+            )
             out_view = out[g].rearrange("(p j) o -> p (j o)", j=ROW_TILES)
-            for half in range(HALVES):
-                adj_t_ps = psum_t.tile([P, BANK], F32, tag="transposed")
-                for k in range(TILES_PER_HALF * 2):
-                    src = (half * TILES_PER_HALF * 2 + k) * P
-                    nc.tensor.transpose(
-                        adj_t_ps[:, k * P : (k + 1) * P], adj_words[:, src : src + P], ident[:]
-                    )
-                adj_grouped = per_half.tile([P, TILES_PER_HALF * P * PACK], BF16, align_bytes=64)
-                nc.scalar.copy(
-                    out=adj_grouped[:].bitcast(F32).rearrange("p (j c u) -> p j c u", j=TILES_PER_HALF, u=2),
-                    in_=adj_t_ps[:].rearrange("p (j u c) -> p j c u", j=TILES_PER_HALF, u=2),
-                )
-                adj_codes = per_half.tile([P, TILES_PER_HALF * P], U32, align_bytes=64)
-                adj_scales = per_half.tile([P, TILES_PER_HALF * P], U8, align_bytes=64)
-                nc.vector.quantize_mx(
-                    out=adj_codes[:].bitcast(FP8X4), scales=adj_scales[:], in_=adj_grouped[:]
-                )
-
-                a_ps = psum_acc.tile([P, TILES_PER_HALF * F_OUT], F32, tag="acc")
-                for j in range(TILES_PER_HALF):
-                    nc.tensor.matmul_mx(
-                        out=a_ps[:, j * F_OUT : (j + 1) * F_OUT],
-                        lhsT=adj_codes[:, j * P : (j + 1) * P].bitcast(FP8X4),
-                        lhsT_scale=adj_scales[:, j * P : (j + 1) * P],
-                        rhs=h_codes_of[g][:].bitcast(FP8X4),
-                        rhs_scale=h_scales_of[g][:],
-                        start=True,
-                        stop=True,
-                    )
-
-                neg_part = per_half.tile([P, TILES_PER_HALF * F_OUT], F32)
-                nc.scalar.activation(out=neg_part[:], in_=a_ps[:], func=ACT.Relu, scale=-1.0)
-                result = per_half.tile([P, TILES_PER_HALF * F_OUT], F32)
-                nc.vector.scalar_tensor_tensor(
-                    out=result[:],
-                    in0=neg_part[:],
-                    scalar=one_minus_alpha[:, 0:1],
-                    in1=a_ps[:],
-                    op0=ALU.mult,
-                    op1=ALU.add,
-                )
-                cols = slice(half * TILES_PER_HALF * F_OUT, (half + 1) * TILES_PER_HALF * F_OUT)
-                nc.sync.dma_start(out=out_view[:, cols], in_=result[:])
+            first = (k % 2) * TILES_PER_HALF * F_OUT
+            nc.sync.dma_start(out=out_view[:, first : first + TILES_PER_HALF * F_OUT], in_=result[:])

@@ -60,8 +60,10 @@ def tile_gcn_s_kernel(tc, seq, adj, W, b, alpha, out):
 
         w_rows = const.tile([P, F_IN], BF16)
         nc.sync.dma_start(out=w_rows[:], in_=W[:, :])
-        nc.scalar.dma_start(out=small_row[0:1, 0:F_OUT], in_=b.unsqueeze(0))
-        nc.scalar.dma_start(out=small_row[0:1, F_OUT : F_OUT + 1], in_=alpha.unsqueeze(0))
+        small_in = const.tile([1, F_OUT + 1], BF16)
+        nc.scalar.dma_start(out=small_in[:, 0:F_OUT], in_=b.unsqueeze(0))
+        nc.scalar.dma_start(out=small_in[:, F_OUT : F_OUT + 1], in_=alpha.unsqueeze(0))
+        nc.vector.tensor_copy(out=small_row[0:1, 0 : F_OUT + 1], in_=small_in[:])
 
         seq_rows_of = []
         for g in range(GRAPHS):

@@ -15,8 +15,8 @@ P = 128
 PACK = 4
 GRAPHS, NODES, F_IN, F_OUT = 2, 512, 256, 128
 ROW_TILES = NODES // P
-TILES_PER_HALF = 2
-HALVES = GRAPHS * ROW_TILES // TILES_PER_HALF
+HALVES = 2 * GRAPHS
+TILES_PER_HALF = ROW_TILES // 2
 BANK = 512
 WARM_PASSES = 12
 
@@ -60,17 +60,16 @@ def tile_gcn_s_kernel(tc, seq, adj, W, b, alpha, out):
 
         w_rows = const.tile([P, F_IN], BF16)
         nc.sync.dma_start(out=w_rows[:], in_=W[:, :])
-        small_in = const.tile([1, F_OUT + 1], BF16)
-        nc.scalar.dma_start(out=small_in[:, 0:F_OUT], in_=b.unsqueeze(0))
-        nc.scalar.dma_start(out=small_in[:, F_OUT : F_OUT + 1], in_=alpha.unsqueeze(0))
-        nc.vector.tensor_copy(out=small_row[0:1, 0 : F_OUT + 1], in_=small_in[:])
+        nc.scalar.dma_start(out=small_row[0:1, 0:F_OUT], in_=b.unsqueeze(0))
+        nc.scalar.dma_start(out=small_row[0:1, F_OUT : F_OUT + 1], in_=alpha.unsqueeze(0))
 
         seq_rows_of = []
-        for g in range(GRAPHS):
-            seq_rows = per_graph.tile([P, PACK * F_IN], BF16)
+        for k in range(HALVES):
+            seq_rows = per_half.tile([P, 2 * F_IN], BF16)
+            first = (k % 2) * (NODES // 2)
             nc.sync.dma_start(
-                out=seq_rows[:].rearrange("p (u r) -> p u r", u=2),
-                in_=seq[g].rearrange("(u p e) i -> p u (e i)", u=2, e=2),
+                out=seq_rows[:],
+                in_=seq[k // 2][first : first + NODES // 2, :].rearrange("(p e) i -> p (e i)", e=2),
             )
             seq_rows_of.append(seq_rows)
 
@@ -94,17 +93,17 @@ def tile_gcn_s_kernel(tc, seq, adj, W, b, alpha, out):
         w_pairs = w_t[:].bitcast(BF16).rearrange("p (o r) -> p o r", r=2)
 
         seq_t_of = []
-        for g in range(GRAPHS):
-            seq_words = seq_rows_of[g][:].bitcast(F32)
+        for k in range(HALVES):
+            seq_words = seq_rows_of[k][:].bitcast(F32)
             seq_t_ps = psum_t.tile([P, BANK], F32, tag="transposed")
-            for t in range(PACK):
-                cols = slice(t * P, (t + 1) * P)
+            for e in range(2):
+                cols = slice(e * P, (e + 1) * P)
                 nc.tensor.transpose(seq_t_ps[:, cols], seq_words[:, cols], ident[:])
-            seq_t = per_graph.tile([P, PACK * P], F32)
-            if g == 0:
-                nc.vector.tensor_copy(out=seq_t[:], in_=seq_t_ps[:])
+            seq_t = per_half.tile([P, 2 * P], F32)
+            if k % 2 == 0:
+                nc.vector.tensor_copy(out=seq_t[:], in_=seq_t_ps[:, 0 : 2 * P])
             else:
-                nc.scalar.copy(out=seq_t[:], in_=seq_t_ps[:])
+                nc.scalar.copy(out=seq_t[:], in_=seq_t_ps[:, 0 : 2 * P])
             seq_t_of.append(seq_t)
 
         small_ps = psum_small.tile([P, 2 * F_OUT], F32)
@@ -129,13 +128,15 @@ def tile_gcn_s_kernel(tc, seq, adj, W, b, alpha, out):
         adj_scales_of = []
 
         def project(g):
-            seq_pairs = seq_t_of[g][:].bitcast(BF16).rearrange("p (t c r) -> p t c r", t=PACK, r=2)
             h_ps = psum_acc.tile([P, PACK * F_OUT], F32, tag="acc")
             for t in range(PACK):
+                seq_pairs = seq_t_of[2 * g + t // 2][:].bitcast(BF16).rearrange(
+                    "p (e c r) -> p e c r", e=2, r=2
+                )
                 for r in range(2):
                     nc.tensor.matmul(
                         h_ps[:, t * F_OUT : (t + 1) * F_OUT],
-                        lhsT=seq_pairs[:, t, :, r],
+                        lhsT=seq_pairs[:, t % 2, :, r],
                         rhs=w_pairs[:, :, r],
                         start=(r == 0),
                         stop=(r == 1),
@@ -162,16 +163,7 @@ def tile_gcn_s_kernel(tc, seq, adj, W, b, alpha, out):
             )
             adj_grouped_of.append(adj_grouped)
 
-        def quantise_h(g):
-            h_codes = per_graph.tile([P, F_OUT], U32, align_bytes=64)
-            h_scales = per_graph.tile([P, F_OUT], U8, align_bytes=64)
-            nc.vector.quantize_mx(
-                out=h_codes[:].bitcast(FP8X4), scales=h_scales[:], in_=h_grouped_of[g][:]
-            )
-            h_codes_of.append(h_codes)
-            h_scales_of.append(h_scales)
-
-        def quantise_adj(k):
+        def quantise(k):
             adj_codes = per_half.tile([P, TILES_PER_HALF * P], U32, align_bytes=64)
             adj_scales = per_half.tile([P, TILES_PER_HALF * P], U8, align_bytes=64)
             nc.vector.quantize_mx(
@@ -179,16 +171,22 @@ def tile_gcn_s_kernel(tc, seq, adj, W, b, alpha, out):
             )
             adj_codes_of.append(adj_codes)
             adj_scales_of.append(adj_scales)
+            if k % 2 == 0:
+                h_codes = per_graph.tile([P, F_OUT], U32, align_bytes=64)
+                h_scales = per_graph.tile([P, F_OUT], U8, align_bytes=64)
+                nc.vector.quantize_mx(
+                    out=h_codes[:].bitcast(FP8X4), scales=h_scales[:], in_=h_grouped_of[k // 2][:]
+                )
+                h_codes_of.append(h_codes)
+                h_scales_of.append(h_scales)
 
         for k in range(HALVES):
-            if k < GRAPHS:
-                project(k)
+            if k % 2 == 0:
+                project(k // 2)
             transpose_adj(k)
             if k >= 1:
-                if k - 1 < GRAPHS:
-                    quantise_h(k - 1)
-                quantise_adj(k - 1)
-        quantise_adj(HALVES - 1)
+                quantise(k - 1)
+        quantise(HALVES - 1)
 
         for k in range(HALVES):
             g = k // 2

from contextlib import ExitStack

import concourse.mybir as mybir
from concourse.masks import make_identity

F32 = mybir.dt.float32
BF16 = mybir.dt.bfloat16
U32 = mybir.dt.uint32
U8 = mybir.dt.uint8
FP8X4 = mybir.dt.float8_e4m3fn_x4
ALU = mybir.AluOpType
ACT = mybir.ActivationFunctionType

P = 128
PACK = 4
GRAPHS, NODES, F_IN, F_OUT = 2, 512, 256, 128
ROW_TILES = NODES // P
HALVES = 2 * GRAPHS
TILES_PER_HALF = ROW_TILES // 2
BANK = 512
WARM_PASSES = 12

FLOPS = 2 * GRAPHS * NODES * F_IN * F_OUT + 2 * GRAPHS * NODES * NODES * F_OUT


def tile_gcn_s_kernel(tc, seq, adj, W, b, alpha, out):
    nc = tc.nc
    with ExitStack() as ctx:
        ctx.enter_context(tc.manual_schedule())
        const = ctx.enter_context(tc.tile_pool(name="const", bufs=1))
        per_graph = ctx.enter_context(tc.tile_pool(name="per_graph", bufs=GRAPHS))
        per_half = ctx.enter_context(tc.tile_pool(name="per_half", bufs=HALVES))
        psum_t = ctx.enter_context(tc.psum_pool(name="psum_t", bufs=3))
        psum_acc = ctx.enter_context(tc.psum_pool(name="psum_acc", bufs=4))
        psum_small = ctx.enter_context(tc.psum_pool(name="psum_small", bufs=1))

        small_row = const.tile([P, 2 * F_OUT], BF16)
        nc.gpsimd.memset(small_row[:], 0.0)
        zero_col = const.tile([P, 1], F32)
        nc.gpsimd.memset(zero_col[:], 0.0)
        ident = const.tile([P, P], F32)
        make_identity(nc, ident[:])

        warm_zeros = const.tile([P, P * PACK], BF16, align_bytes=64)
        nc.vector.memset(warm_zeros[:], 0.0)
        warm_codes = const.tile([P, P], U32, align_bytes=64)
        warm_scales = const.tile([P, P], U8, align_bytes=64)
        nc.vector.quantize_mx(out=warm_codes[:].bitcast(FP8X4), scales=warm_scales[:], in_=warm_zeros[:])
        warm_ps = psum_t.tile([P, BANK], F32, tag="transposed")
        for i in range(WARM_PASSES):
            nc.tensor.matmul_mx(
                out=warm_ps[:, 0:P],
                lhsT=warm_codes[:].bitcast(FP8X4),
                lhsT_scale=warm_scales[:],
                rhs=warm_codes[:].bitcast(FP8X4),
                rhs_scale=warm_scales[:],
                start=True,
                stop=True,
            )

        w_rows = const.tile([P, F_IN], BF16)
        nc.sync.dma_start(out=w_rows[:], in_=W[:, :])
        nc.scalar.dma_start(out=small_row[0:1, 0:F_OUT], in_=b.unsqueeze(0))
        nc.scalar.dma_start(out=small_row[0:1, F_OUT : F_OUT + 1], in_=alpha.unsqueeze(0))

        seq_rows_of = []
        for k in range(HALVES):
            seq_rows = per_half.tile([P, 2 * F_IN], BF16)
            first = (k % 2) * (NODES // 2)
            nc.sync.dma_start(
                out=seq_rows[:],
                in_=seq[k // 2][first : first + NODES // 2, :].rearrange("(p e) i -> p (e i)", e=2),
            )
            seq_rows_of.append(seq_rows)

        adj_rows_of = []
        for k in range(HALVES):
            adj_rows = per_half.tile([P, TILES_PER_HALF * NODES], BF16)
            adj_view = adj[k // 2].rearrange("(p j) m -> p (j m)", j=ROW_TILES)
            first = (k % 2) * TILES_PER_HALF * NODES
            nc.sync.dma_start(out=adj_rows[:], in_=adj_view[:, first : first + TILES_PER_HALF * NODES])
            adj_rows_of.append(adj_rows)

        ones = const.tile([P, P], BF16)
        nc.scalar.activation(
            out=ones[:], in_=zero_col[:, 0:1].to_broadcast([P, P]), func=ACT.Relu, scale=0.0, bias=1.0
        )

        w_t_ps = psum_t.tile([P, BANK], F32, tag="transposed")
        nc.tensor.transpose(w_t_ps[:, 0:P], w_rows[:].bitcast(F32), ident[:])
        w_t = const.tile([P, F_OUT], F32)
        nc.scalar.copy(out=w_t[:], in_=w_t_ps[:, 0:P])
        w_pairs = w_t[:].bitcast(BF16).rearrange("p (o r) -> p o r", r=2)

        seq_t_of = []
        for k in range(HALVES):
            seq_words = seq_rows_of[k][:].bitcast(F32)
            seq_t_ps = psum_t.tile([P, BANK], F32, tag="transposed")
            for e in range(2):
                cols = slice(e * P, (e + 1) * P)
                nc.tensor.transpose(seq_t_ps[:, cols], seq_words[:, cols], ident[:])
            seq_t = per_half.tile([P, 2 * P], F32)
            if k % 2 == 0:
                nc.vector.tensor_copy(out=seq_t[:], in_=seq_t_ps[:, 0 : 2 * P])
            else:
                nc.scalar.copy(out=seq_t[:], in_=seq_t_ps[:, 0 : 2 * P])
            seq_t_of.append(seq_t)

        small_ps = psum_small.tile([P, 2 * F_OUT], F32)
        nc.tensor.matmul(small_ps[:], lhsT=ones[:], rhs=small_row[:], start=True, stop=True)
        bias_all = const.tile([P, F_OUT], F32)
        nc.vector.tensor_copy(out=bias_all[:], in_=small_ps[:, 0:F_OUT])
        one_minus_alpha = const.tile([P, 1], F32)
        nc.vector.tensor_scalar(
            out=one_minus_alpha[:],
            in0=small_ps[:, F_OUT : F_OUT + 1],
            scalar1=-1.0,
            scalar2=1.0,
            op0=ALU.mult,
            op1=ALU.add,
        )

        h_grouped_of = []
        h_codes_of = []
        h_scales_of = []
        adj_grouped_of = []
        adj_codes_of = []
        adj_scales_of = []

        def project(g):
            h_ps = psum_acc.tile([P, PACK * F_OUT], F32, tag="acc")
            for t in range(PACK):
                seq_pairs = seq_t_of[2 * g + t // 2][:].bitcast(BF16).rearrange(
                    "p (e c r) -> p e c r", e=2, r=2
                )
                for r in range(2):
                    nc.tensor.matmul(
                        h_ps[:, t * F_OUT : (t + 1) * F_OUT],
                        lhsT=seq_pairs[:, t % 2, :, r],
                        rhs=w_pairs[:, :, r],
                        start=(r == 0),
                        stop=(r == 1),
                    )
            h_grouped = per_graph.tile([P, F_OUT * PACK], BF16, align_bytes=64)
            nc.vector.tensor_tensor(
                out=h_grouped[:].rearrange("p (o t) -> p o t", t=PACK),
                in0=h_ps[:].rearrange("p (t o) -> p o t", t=PACK),
                in1=bias_all[:].unsqueeze(2).to_broadcast([P, F_OUT, PACK]),
                op=ALU.add,
            )
            h_grouped_of.append(h_grouped)

        def transpose_adj(k):
            adj_words = adj_rows_of[k][:].bitcast(F32)
            adj_t_ps = psum_t.tile([P, BANK], F32, tag="transposed")
            for block in range(TILES_PER_HALF * 2):
                cols = slice(block * P, (block + 1) * P)
                nc.tensor.transpose(adj_t_ps[:, cols], adj_words[:, cols], ident[:])
            adj_grouped = per_half.tile([P, TILES_PER_HALF * P * PACK], BF16, align_bytes=64)
            nc.scalar.copy(
                out=adj_grouped[:].bitcast(F32).rearrange("p (j c u) -> p j c u", j=TILES_PER_HALF, u=2),
                in_=adj_t_ps[:].rearrange("p (j u c) -> p j c u", j=TILES_PER_HALF, u=2),
            )
            adj_grouped_of.append(adj_grouped)

        def quantise(k):
            adj_codes = per_half.tile([P, TILES_PER_HALF * P], U32, align_bytes=64)
            adj_scales = per_half.tile([P, TILES_PER_HALF * P], U8, align_bytes=64)
            nc.vector.quantize_mx(
                out=adj_codes[:].bitcast(FP8X4), scales=adj_scales[:], in_=adj_grouped_of[k][:]
            )
            adj_codes_of.append(adj_codes)
            adj_scales_of.append(adj_scales)
            if k % 2 == 0:
                h_codes = per_graph.tile([P, F_OUT], U32, align_bytes=64)
                h_scales = per_graph.tile([P, F_OUT], U8, align_bytes=64)
                nc.vector.quantize_mx(
                    out=h_codes[:].bitcast(FP8X4), scales=h_scales[:], in_=h_grouped_of[k // 2][:]
                )
                h_codes_of.append(h_codes)
                h_scales_of.append(h_scales)

        for k in range(HALVES):
            if k % 2 == 0:
                project(k // 2)
            transpose_adj(k)
            if k >= 1:
                quantise(k - 1)
        quantise(HALVES - 1)

        for k in range(HALVES):
            g = k // 2
            a_ps = psum_acc.tile([P, TILES_PER_HALF * F_OUT], F32, tag="acc")
            for j in range(TILES_PER_HALF):
                nc.tensor.matmul_mx(
                    out=a_ps[:, j * F_OUT : (j + 1) * F_OUT],
                    lhsT=adj_codes_of[k][:, j * P : (j + 1) * P].bitcast(FP8X4),
                    lhsT_scale=adj_scales_of[k][:, j * P : (j + 1) * P],
                    rhs=h_codes_of[g][:].bitcast(FP8X4),
                    rhs_scale=h_scales_of[g][:],
                    start=True,
                    stop=True,
                )
            neg_part = per_half.tile([P, TILES_PER_HALF * F_OUT], F32)
            nc.scalar.activation(out=neg_part[:], in_=a_ps[:], func=ACT.Relu, scale=-1.0)
            result = per_half.tile([P, TILES_PER_HALF * F_OUT], F32)
            nc.vector.scalar_tensor_tensor(
                out=result[:],
                in0=neg_part[:],
                scalar=one_minus_alpha[:, 0:1],
                in1=a_ps[:],
                op0=ALU.mult,
                op1=ALU.add,
            )
            out_view = out[g].rearrange("(p j) o -> p (j o)", j=ROW_TILES)
            first = (k % 2) * TILES_PER_HALF * F_OUT
            nc.sync.dma_start(out=out_view[:, first : first + TILES_PER_HALF * F_OUT], in_=result[:])
